import numpy as np
import ml_dtypes


def mxq(x, axis, fmt="e4m3"):
    dtype, down = {"e4m3": (ml_dtypes.float8_e4m3fn, 7), "e5m2": (ml_dtypes.float8_e5m2, 14)}[fmt]
    v = np.moveaxis(np.asarray(x, np.float32).astype(ml_dtypes.bfloat16).astype(np.float64), axis, -1)
    blocks = v.reshape(v.shape[:-1] + (-1, 32))
    amax = np.abs(blocks).max(-1, keepdims=True)
    byte = np.maximum(np.where(amax > 0, np.frexp(amax)[1] - 1 + 127, 0) - down, 1)
    scale = np.exp2(byte - 127.0)
    codes = (blocks / scale).astype(np.float32).astype(dtype).astype(np.float64)
    return np.moveaxis((codes * scale).reshape(v.shape), -1, axis)


WIDE = False


def mx_kscale(k):
    if not WIDE:
        return np.ones(k)
    levels = np.array([10, -10, 5, -5, 0])
    if k % 512:
        return np.exp2(np.random.permutation(np.resize(levels, k // 32))).repeat(32)
    a = np.empty((k // 512, 16))
    for p in range(k // 512):
        a[p, :8] = np.random.permutation(np.resize(levels, 8))
        for g in range(8):
            far = levels[np.abs(levels - a[p, g]) >= 10]
            a[p, g + 8] = far[np.random.randint(len(far))]
    return np.exp2(a.ravel()).repeat(32)


BF16 = ml_dtypes.bfloat16


def bf(x):
    return np.asarray(x, np.float32).astype(BF16)


def f64(x):
    return np.asarray(x).astype(np.float64)


B, T, C, KW = 2, 1024, 512, 3
PAD = KW // 2


def setup_inputs():
    s = mx_kscale(C)
    return {"x": bf(np.random.standard_normal((B, T, C)) * s),
            "w1": bf(np.random.standard_normal((C, C)) / np.sqrt(C) / s[None, :]),
            "b1": bf(np.random.standard_normal(C) * 0.2),
            "w2": bf(np.random.standard_normal((C, KW)) * 0.8),
            "b2": bf(np.random.standard_normal(C) * 0.2)}


def core(x, w1, b1, w2, b2):
    h = (mxq(f64(x), 2, "e4m3") @ mxq(f64(w1), 1, "e4m3").T) + f64(b1)
    hp = np.pad(h, ((0, 0), (PAD, PAD), (0, 0)))
    taps = f64(w2)
    y = hp[:, 0:T, :] * taps[:, 0]
    for j in range(1, KW):
        y = y + hp[:, j:j + T, :] * taps[:, j]
    return y + f64(b2)


def e4m3fn_bytes(y):
    return np.clip(np.asarray(y, np.float64), -448.0, 448.0).astype(np.float32).astype(ml_dtypes.float8_e4m3fn).view(np.uint8)


def reference(x, w1, b1, w2, b2):
    out = core(x, w1, b1, w2, b2)
    s = np.max(np.abs(out), axis=-1, keepdims=True) / 448.0
    return out, e4m3fn_bytes(out / s)

@@ -1,0 +1,266 @@
+from contextlib import ExitStack
+
+import concourse.mybir as mybir
+from concourse.masks import make_identity
+
+F32 = mybir.dt.float32
+BF16 = mybir.dt.bfloat16
+U32 = mybir.dt.uint32
+U8 = mybir.dt.uint8
+FP8X4 = mybir.dt.float8_e4m3fn_x4
+FP8 = mybir.dt.float8_e4m3fn
+ALU = mybir.AluOpType
+ACT = mybir.ActivationFunctionType
+AX = mybir.AxisListType
+
+B, T, C, KW = 2, 1024, 512, 3
+P = 128
+NDT = C // P
+CH = 512
+NCH = B * T // CH
+PITCH = 1040
+OFF0 = 8
+FLOPS = 2 * B * T * C * C + 2 * KW * B * T * C
+
+WARM = 6
+STREAM = True
+HB = 3
+TPB = 5
+S_CAST = (11, 12, 14)
+V_P0 = ((0, 1), (1, 1), (2, 1))
+PREP_ENG = ("", "vs", "ss", "ss")
+SUBS = (
+    (0, 0, 512, (0, 1, 2)),
+    (0, 512, 512, (3, 4, 5, 6, 7)),
+    (1, 0, 512, (8, 9, 10)),
+    (1, 512, 512, (11, 12, 13, 14, 15)),
+)
+
+
+def tile_cvim_pa_kernel(tc, x, w1, b1, w2, b2, out_0, out_1):
+    nc = tc.nc
+    xf = x.flatten_outer_dims()
+    o0f = out_0.flatten_outer_dims()
+    o1f = out_1.flatten_outer_dims()
+
+    with ExitStack() as ctx:
+        keep = ctx.enter_context(tc.tile_pool(name="keep", bufs=1))
+        work = ctx.enter_context(tc.tile_pool(name="work", bufs=4))
+        psum = ctx.enter_context(tc.psum_pool(name="psum", bufs=2))
+
+        def load_w(h):
+            raw = keep.tile([P, 2, C], BF16, name="wraw%d" % h)
+            nc.sync.dma_start(out=raw[:], in_=w1.rearrange("(p c) k -> p c k", c=NDT)[:, 2 * h:2 * h + 2, :])
+            return raw
+
+        def load_x(i):
+            raw = keep.tile([P, 2, C], BF16, name="xraw%d" % i)
+            nc.sync.dma_start(out=raw[:], in_=xf[256 * i:256 * (i + 1), :].rearrange("(p a) k -> p a k", a=2))
+            return raw
+
+        w_raw = [None, None]
+        x_raw = [None] * 8
+        w_raw[0] = load_w(0)
+        x_raw[0] = load_x(0)
+        w_raw[1] = load_w(1)
+        x_raw[1] = load_x(1)
+
+        b1c = keep.tile([P, NDT, 1], BF16, name="b1c")
+        b2c = keep.tile([P, NDT, 1], BF16, name="b2c")
+        w2c = keep.tile([P, NDT, KW], BF16, name="w2c")
+        nc.scalar.dma_start(out=b1c[:], in_=b1.rearrange("(p c o) -> p c o", c=NDT, o=1))
+        nc.scalar.dma_start(out=w2c[:], in_=w2.rearrange("(p c) j -> p c j", c=NDT))
+        nc.scalar.dma_start(out=b2c[:], in_=b2.rearrange("(p c o) -> p c o", c=NDT, o=1))
+        for i in range(2, 8):
+            x_raw[i] = load_x(i)
+
+        if WARM:
+            wz = keep.tile([P, CH], BF16, name="wz")
+            nc.vector.memset(wz[:], 0.0)
+            dm = psum.tile([P, CH], F32, tag="tp", bufs=TPB, name="dm")
+            for i in range(WARM):
+                nc.tensor.matmul(dm[:], lhsT=wz[:, 0:P], rhs=wz[:], start=True, stop=True)
+
+        ident = keep.tile([P, P], F32, name="ident")
+        make_identity(nc, ident[:])
+        zt = keep.tile([P, 1], F32, name="zt")
+        nc.vector.memset(zt[:], 0.0)
+        junk = keep.tile([P, 1], F32, name="junk")
+        nc.scalar.activation(out=junk[:], in_=zt[:], func=ACT.Identity, bias=zt[:, 0:1], scale=1.0)
+
+        b1f = keep.tile([P, NDT, 1], F32, name="b1f")
+        b2f = keep.tile([P, NDT, 1], F32, name="b2f")
+        w2f = keep.tile([P, NDT, KW], F32, name="w2f")
+        nc.vector.tensor_copy(out=b1f[:], in_=b1c[:])
+        nc.vector.tensor_copy(out=w2f[:], in_=w2c[:])
+        nc.vector.tensor_copy(out=b2f[:], in_=b2c[:])
+        c0 = keep.tile([P, NDT, 1], F32, name="c0")
+        w12 = keep.tile([P, NDT, 1], F32, name="w12")
+        c1a = keep.tile([P, NDT, 1], F32, name="c1a")
+        c1 = keep.tile([P, NDT, 1], F32, name="c1")
+        f2 = keep.tile([P, NDT, 1], F32, name="f2")
+        nc.vector.tensor_tensor(out=c0[:], in0=w2f[:, :, 0:1], in1=b1f[:], op=ALU.mult)
+        nc.vector.tensor_tensor(out=w12[:], in0=w2f[:, :, 1:2], in1=w2f[:, :, 2:3], op=ALU.add)
+        nc.vector.tensor_tensor(out=c1a[:], in0=w12[:], in1=b1f[:], op=ALU.mult)
+        nc.vector.tensor_tensor(out=c1[:], in0=c1a[:], in1=b2f[:], op=ALU.add)
+        nc.vector.scalar_tensor_tensor(out=f2[:], in0=w2f[:, :, 2:3], scalar=-1.0, in1=b1f[:], op0=ALU.mult, op1=ALU.mult)
+
+        ys = [keep.tile([P, NDT, T], F32, name="y%d" % b) for b in range(B)]
+        p0s = [keep.tile([P, NDT, PITCH], F32, name="p0_%d" % b) for b in range(B)]
+        for b in range(B):
+            nc.gpsimd.memset(p0s[b][:, :, OFF0 - 1:OFF0], 0.0)
+
+        fixt = keep.tile([P, NDT, P], F32, name="fixt")
+        nc.gpsimd.memset(fixt[:], 0.0)
+        nc.vector.tensor_copy(out=fixt[:, :, P - 1:P], in_=f2[:])
+
+        am = keep.tile([P, 16], F32, name="am")
+        rc = keep.tile([P, 16], F32, name="rc")
+        rs = keep.tile([P, 16], F32, name="rs")
+
+        wq = keep.tile([P, CH], U32, name="wq", align_bytes=64)
+        ws = keep.tile([P, CH], U8, name="ws", align_bytes=64)
+        xq = [keep.tile([P, CH], U32, name="xq%d" % c, align_bytes=64) for c in range(NCH)]
+        xs = [keep.tile([P, CH], U8, name="xs%d" % c, align_bytes=64) for c in range(NCH)]
+
+        def turn(raw):
+            words = raw[:].bitcast(F32)
+            tin = psum.tile([P, 2, 2, P], F32, tag="tp", bufs=TPB, name="tin")
+            for a in range(2):
+                for u in range(2):
+                    nc.tensor.transpose(tin[:, a, u, :], words[:, a, u:C // 2:2], ident[:])
+            return tin
+
+        def gather(tin, dst, eng, order):
+            if order == "w":
+                o = dst.rearrange("p (a r u) -> p a r u", a=2, u=2)
+                i = tin[:].rearrange("p a u r -> p a r u")
+            else:
+                o = dst.rearrange("p (r a u) -> p r a u", a=2, u=2)
+                i = tin[:].rearrange("p a u r -> p r a u")
+            if eng == "s":
+                nc.scalar.copy(out=o, in_=i)
+            else:
+                nc.vector.tensor_copy(out=o, in_=i)
+
+        def quant(g, codes, scales):
+            nc.vector.quantize_mx(out=codes.bitcast(FP8X4), scales=scales, in_=g.bitcast(BF16))
+
+        gw = work.tile([P, 2, CH], F32, tag="g", bufs=3, name="gw", align_bytes=64)
+        g0 = work.tile([P, 2, CH], F32, tag="g", bufs=3, name="g0", align_bytes=64)
+        tw0 = turn(w_raw[0])
+        tx0 = turn(x_raw[0])
+        gather(tw0, gw[:, 0, :], "s", "w")
+        gather(tx0, g0[:, 0, :], "v", "x")
+        tw1 = turn(w_raw[1])
+        tx1 = turn(x_raw[1])
+        quant(gw[:, 0, :], wq[:, 0:256], ws[:, 0:256])
+        quant(g0[:, 0, :], xq[0][:, 0:256], xs[0][:, 0:256])
+        gather(tw1, gw[:, 1, :], "s", "w")
+        gather(tx1, g0[:, 1, :], "v", "x")
+        quant(gw[:, 1, :], wq[:, 256:512], ws[:, 256:512])
+        quant(g0[:, 1, :], xq[0][:, 256:512], xs[0][:, 256:512])
+
+        def prep(c):
+            g = work.tile([P, 2, CH], F32, tag="g", bufs=3, name="g", align_bytes=64)
+            tins = [turn(x_raw[2 * c]), turn(x_raw[2 * c + 1])]
+            for h in range(2):
+                gather(tins[h], g[:, h, :], PREP_ENG[c][h], "x")
+            quant(g[:].rearrange("p h w -> p (h w)"), xq[c][:], xs[c][:])
+
+        def mm(s, d):
+            b, t0, n, tiles = SUBS[s]
+            c, col = divmod(b * T + t0, CH)
+            h = psum.tile([P, CH], F32, tag="h", bufs=HB, name="h")
+            nc.tensor.matmul_mx(
+                out=h[:, 0:n],
+                lhsT=wq[:, d * P:(d + 1) * P].bitcast(FP8X4),
+                lhsT_scale=ws[:, d * P:(d + 1) * P],
+                rhs=xq[c][:, col:col + n].bitcast(FP8X4),
+                rhs_scale=xs[c][:, col:col + n],
+                start=True,
+                stop=True,
+            )
+            return h
+
+        def conv(s, d, h):
+            b, t0, n, tiles = SUBS[s]
+            nc.scalar.activation(out=ys[b][:, d, t0:t0 + n], in_=h[:, 0:n], func=ACT.Identity,
+                                 scale=w2f[:, d, 1:2], bias=c1[:, d, :])
+            dst = p0s[b][:, d, OFF0 + t0:OFF0 + t0 + n]
+            if (s, d) in V_P0:
+                nc.vector.tensor_scalar(out=dst, in0=h[:, 0:n], scalar1=w2f[:, d, 0:1], scalar2=c0[:, d, :],
+                                        op0=ALU.mult, op1=ALU.add)
+            else:
+                nc.scalar.activation(out=dst, in_=h[:, 0:n], func=ACT.Identity, scale=w2f[:, d, 0:1], bias=c0[:, d, :])
+            if t0 == 0:
+                seg = ys[b][:, d, 0:n - 1]
+                src = h[:, 1:n]
+            else:
+                seg = ys[b][:, d, t0 - 1:t0 + n - 1]
+                src = h[:, 0:n]
+            nc.vector.scalar_tensor_tensor(out=seg, in0=src, scalar=w2f[:, d, 2:3], in1=seg, op0=ALU.mult, op1=ALU.add)
+
+        yos = [None] * 16
+        o0s = [None] * 16
+
+        def blocks(k, d):
+            b, t0 = divmod(k * P, T)
+            if d == 0:
+                yos[k] = psum.tile([P, C], F32, tag="tp", bufs=TPB, name="yo")
+            dst = yos[k][:, d * P:(d + 1) * P]
+            st = OFF0 + t0 - 1
+            nc.tensor.matmul(dst, lhsT=p0s[b][:, d, st:st + P], rhs=ident[:], is_transpose=True, start=True, stop=False)
+            last = t0 + P == T
+            nc.tensor.matmul(dst, lhsT=ys[b][:, d, t0:t0 + P], rhs=ident[:], is_transpose=True, start=False, stop=not last)
+            if last:
+                nc.tensor.matmul(dst, lhsT=fixt[:, d, :], rhs=ident[:], is_transpose=True, start=False, stop=True)
+
+        def leave(k):
+            o0 = work.tile([P, C], F32, tag="o0", bufs=10, name="o0")
+            nc.scalar.copy(out=o0[:].rearrange("p (m c) -> p m c", c=NDT), in_=yos[k][:].rearrange("p (c m) -> p m c", c=NDT))
+            nc.sync.dma_start(out=o0f[k * P:(k + 1) * P, :], in_=o0[:])
+            nc.vector.tensor_reduce(out=am[:, k:k + 1], in_=o0[:], axis=AX.X, op=ALU.max, apply_absolute_value=True)
+            o0s[k] = o0
+
+        def finish(tiles):
+            k0, k1 = tiles[0], tiles[-1] + 1
+            nc.vector.reciprocal(out=rc[:, k0:k1], in_=am[:, k0:k1])
+            nc.vector.tensor_scalar(out=rs[:, k0:k1], in0=rc[:, k0:k1], scalar1=448.0, scalar2=None, op0=ALU.mult)
+            for k in tiles:
+                o8 = work.tile([P, C], FP8, tag="o8", bufs=6, name="o8")
+                if k in S_CAST:
+                    nc.scalar.activation(out=o8[:], in_=o0s[k][:], func=ACT.Identity, scale=rs[:, k:k + 1],
+                                         bias=zt[:, 0:1], saturate=False)
+                else:
+                    nc.vector.tensor_scalar(out=o8[:], in0=o0s[k][:], scalar1=rs[:, k:k + 1], scalar2=None,
+                                            op0=ALU.mult, saturate=False)
+                nc.sync.dma_start(out=o1f[k * P:(k + 1) * P, :], in_=o8[:].bitcast(U8))
+
+        NS = len(SUBS)
+        steps = [(s, d) for s in range(NS) for d in range(NDT)]
+        hq = [mm(0, 0), mm(0, 1)]
+        prep(1)
+        for i in range(len(steps)):
+            s, d = steps[i]
+            tiles = SUBS[s][3]
+            if i + 2 < len(steps):
+                hq.append(mm(steps[i + 2][0], steps[i + 2][1]))
+            conv(s, d, hq[i])
+            for k in tiles:
+                blocks(k, d)
+            if s == 0 and d == 1:
+                prep(2)
+            if s == 0 and d == 3:
+                prep(3)
+            if s > 0 and d == 1:
+                finish(SUBS[s - 1][3])
+            if d == NDT - 1 and s < NS - 1:
+                for k in tiles:
+                    leave(k)
+        for k in (11, 12, 13):
+            leave(k)
+        finish((11, 12, 13))
+        for k in (14, 15):
+            leave(k)
+        finish((14, 15))

@@ -23,12 +23,13 @@ OFF0 = 8
 FLOPS = 2 * B * T * C * C + 2 * KW * B * T * C
 
 WARM = 6
+LAG = 2
 STREAM = True
 HB = 3
 TPB = 5
 S_CAST = (11, 12, 14)
-V_P0 = ((0, 1), (1, 1), (2, 1))
 PREP_ENG = ("", "vs", "ss", "ss")
+G_SLOT = {0: 0, 2: 1}
 SUBS = (
     (0, 0, 512, (0, 1, 2)),
     (0, 512, 512, (3, 4, 5, 6, 7)),
@@ -60,10 +61,10 @@ def tile_cvim_pa_kernel(tc, x, w1, b1, w2, b2, out_0, out_1):
 
         w_raw = [None, None]
         x_raw = [None] * 8
-        w_raw[0] = load_w(0)
         x_raw[0] = load_x(0)
-        w_raw[1] = load_w(1)
+        w_raw[0] = load_w(0)
         x_raw[1] = load_x(1)
+        w_raw[1] = load_w(1)
 
         b1c = keep.tile([P, NDT, 1], BF16, name="b1c")
         b2c = keep.tile([P, NDT, 1], BF16, name="b2c")
@@ -104,11 +105,15 @@ def tile_cvim_pa_kernel(tc, x, w1, b1, w2, b2, out_0, out_1):
         nc.vector.tensor_tensor(out=c1a[:], in0=w12[:], in1=b1f[:], op=ALU.mult)
         nc.vector.tensor_tensor(out=c1[:], in0=c1a[:], in1=b2f[:], op=ALU.add)
         nc.vector.scalar_tensor_tensor(out=f2[:], in0=w2f[:, :, 2:3], scalar=-1.0, in1=b1f[:], op0=ALU.mult, op1=ALU.mult)
+        c1p = keep.tile([P, NDT, 1], F32, name="c1p")
+        nc.vector.tensor_tensor(out=c1p[:], in0=c1[:], in1=f2[:], op=ALU.add)
 
         ys = [keep.tile([P, NDT, T], F32, name="y%d" % b) for b in range(B)]
         p0s = [keep.tile([P, NDT, PITCH], F32, name="p0_%d" % b) for b in range(B)]
+        p2s = [keep.tile([P, len(G_SLOT), T + 8], F32, name="p2_%d" % b) for b in range(B)]
         for b in range(B):
             nc.gpsimd.memset(p0s[b][:, :, OFF0 - 1:OFF0], 0.0)
+            nc.gpsimd.memset(p2s[b][:, :, T:T + 1], 0.0)
 
         fixt = keep.tile([P, NDT, P], F32, name="fixt")
         nc.gpsimd.memset(fixt[:], 0.0)
@@ -148,18 +153,19 @@ def tile_cvim_pa_kernel(tc, x, w1, b1, w2, b2, out_0, out_1):
 
         gw = work.tile([P, 2, CH], F32, tag="g", bufs=3, name="gw", align_bytes=64)
         g0 = work.tile([P, 2, CH], F32, tag="g", bufs=3, name="g0", align_bytes=64)
-        tw0 = turn(w_raw[0])
+        ctx.enter_context(tc.manual_schedule(engines={mybir.EngineType.PE}))
         tx0 = turn(x_raw[0])
-        gather(tw0, gw[:, 0, :], "s", "w")
+        tw0 = turn(w_raw[0])
         gather(tx0, g0[:, 0, :], "v", "x")
-        tw1 = turn(w_raw[1])
+        gather(tw0, gw[:, 0, :], "s", "w")
         tx1 = turn(x_raw[1])
-        quant(gw[:, 0, :], wq[:, 0:256], ws[:, 0:256])
+        tw1 = turn(w_raw[1])
         quant(g0[:, 0, :], xq[0][:, 0:256], xs[0][:, 0:256])
+        quant(gw[:, 0, :], wq[:, 0:256], ws[:, 0:256])
+        gather(tx1, g0[:, 1, :], "s", "x")
         gather(tw1, gw[:, 1, :], "s", "w")
-        gather(tx1, g0[:, 1, :], "v", "x")
-        quant(gw[:, 1, :], wq[:, 256:512], ws[:, 256:512])
         quant(g0[:, 1, :], xq[0][:, 256:512], xs[0][:, 256:512])
+        quant(gw[:, 1, :], wq[:, 256:512], ws[:, 256:512])
 
         def prep(c):
             g = work.tile([P, 2, CH], F32, tag="g", bufs=3, name="g", align_bytes=64)
@@ -185,14 +191,20 @@ def tile_cvim_pa_kernel(tc, x, w1, b1, w2, b2, out_0, out_1):
 
         def conv(s, d, h):
             b, t0, n, tiles = SUBS[s]
+            dst = p0s[b][:, d, OFF0 + t0:OFF0 + t0 + n]
+            if d in G_SLOT:
+                hs = work.tile([P, CH], F32, tag="hs", bufs=4, name="hs")
+                nc.scalar.activation(out=hs[:, 0:n], in_=h[:, 0:n], func=ACT.Identity, scale=1.0, bias=b1f[:, d, :])
+                nc.vector.tensor_scalar(out=ys[b][:, d, t0:t0 + n], in0=h[:, 0:n], scalar1=w2f[:, d, 1:2],
+                                        scalar2=c1p[:, d, :], op0=ALU.mult, op1=ALU.add)
+                nc.gpsimd.tensor_scalar(out=dst, in0=hs[:, 0:n], scalar1=w2f[:, d, 0:1], scalar2=zt[:, 0:1],
+                                        op0=ALU.mult, op1=ALU.add)
+                nc.gpsimd.tensor_scalar(out=p2s[b][:, G_SLOT[d], t0:t0 + n], in0=hs[:, 0:n], scalar1=w2f[:, d, 2:3],
+                                        scalar2=zt[:, 0:1], op0=ALU.mult, op1=ALU.add)
+                return
             nc.scalar.activation(out=ys[b][:, d, t0:t0 + n], in_=h[:, 0:n], func=ACT.Identity,
                                  scale=w2f[:, d, 1:2], bias=c1[:, d, :])
-            dst = p0s[b][:, d, OFF0 + t0:OFF0 + t0 + n]
-            if (s, d) in V_P0:
-                nc.vector.tensor_scalar(out=dst, in0=h[:, 0:n], scalar1=w2f[:, d, 0:1], scalar2=c0[:, d, :],
-                                        op0=ALU.mult, op1=ALU.add)
-            else:
-                nc.scalar.activation(out=dst, in_=h[:, 0:n], func=ACT.Identity, scale=w2f[:, d, 0:1], bias=c0[:, d, :])
+            nc.scalar.activation(out=dst, in_=h[:, 0:n], func=ACT.Identity, scale=w2f[:, d, 0:1], bias=c0[:, d, :])
             if t0 == 0:
                 seg = ys[b][:, d, 0:n - 1]
                 src = h[:, 1:n]
@@ -211,6 +223,11 @@ def tile_cvim_pa_kernel(tc, x, w1, b1, w2, b2, out_0, out_1):
             dst = yos[k][:, d * P:(d + 1) * P]
             st = OFF0 + t0 - 1
             nc.tensor.matmul(dst, lhsT=p0s[b][:, d, st:st + P], rhs=ident[:], is_transpose=True, start=True, stop=False)
+            if d in G_SLOT:
+                nc.tensor.matmul(dst, lhsT=ys[b][:, d, t0:t0 + P], rhs=ident[:], is_transpose=True, start=False, stop=False)
+                nc.tensor.matmul(dst, lhsT=p2s[b][:, G_SLOT[d], t0 + 1:t0 + 1 + P], rhs=ident[:], is_transpose=True,
+                                 start=False, stop=True)
+                return
             last = t0 + P == T
             nc.tensor.matmul(dst, lhsT=ys[b][:, d, t0:t0 + P], rhs=ident[:], is_transpose=True, start=False, stop=not last)
             if last:
@@ -239,25 +256,28 @@ def tile_cvim_pa_kernel(tc, x, w1, b1, w2, b2, out_0, out_1):
 
         NS = len(SUBS)
         steps = [(s, d) for s in range(NS) for d in range(NDT)]
-        hq = [mm(0, 0), mm(0, 1)]
         prep(1)
-        for i in range(len(steps)):
-            s, d = steps[i]
-            tiles = SUBS[s][3]
+        hq = [mm(0, 0), mm(0, 1)]
+        for i in range(len(steps) + LAG):
             if i + 2 < len(steps):
                 hq.append(mm(steps[i + 2][0], steps[i + 2][1]))
-            conv(s, d, hq[i])
-            for k in tiles:
-                blocks(k, d)
-            if s == 0 and d == 1:
-                prep(2)
-            if s == 0 and d == 3:
-                prep(3)
-            if s > 0 and d == 1:
-                finish(SUBS[s - 1][3])
-            if d == NDT - 1 and s < NS - 1:
+            if i < len(steps):
+                s, d = steps[i]
+                conv(s, d, hq[i])
+                if s == 0 and d == 1:
+                    prep(2)
+                if s == 0 and d == 3:
+                    prep(3)
+            if i >= LAG:
+                s, d = steps[i - LAG]
+                tiles = SUBS[s][3]
                 for k in tiles:
-                    leave(k)
+                    blocks(k, d)
+                if s > 0 and d == 1:
+                    finish(SUBS[s - 1][3])
+                if d == NDT - 1 and s < NS - 1:
+                    for k in tiles:
+                        leave(k)
         for k in (11, 12, 13):
             leave(k)
         finish((11, 12, 13))

@@ -27,7 +27,8 @@ LAG = 2
 STREAM = True
 HB = 3
 TPB = 5
-S_CAST = (11, 12, 14)
+S_CAST = (12, 14)
+V_P0 = ((1, 1),)
 PREP_ENG = ("", "vs", "ss", "ss")
 G_SLOT = {0: 0, 2: 1}
 SUBS = (
@@ -110,7 +111,7 @@ def tile_cvim_pa_kernel(tc, x, w1, b1, w2, b2, out_0, out_1):
 
         ys = [keep.tile([P, NDT, T], F32, name="y%d" % b) for b in range(B)]
         p0s = [keep.tile([P, NDT, PITCH], F32, name="p0_%d" % b) for b in range(B)]
-        p2s = [keep.tile([P, len(G_SLOT), T + 8], F32, name="p2_%d" % b) for b in range(B)]
+        p2s = [keep.tile([P, max(1, len(G_SLOT)), T + 8], F32, name="p2_%d" % b) for b in range(B)]
         for b in range(B):
             nc.gpsimd.memset(p0s[b][:, :, OFF0 - 1:OFF0], 0.0)
             nc.gpsimd.memset(p2s[b][:, :, T:T + 1], 0.0)
@@ -204,7 +205,11 @@ def tile_cvim_pa_kernel(tc, x, w1, b1, w2, b2, out_0, out_1):
                 return
             nc.scalar.activation(out=ys[b][:, d, t0:t0 + n], in_=h[:, 0:n], func=ACT.Identity,
                                  scale=w2f[:, d, 1:2], bias=c1[:, d, :])
-            nc.scalar.activation(out=dst, in_=h[:, 0:n], func=ACT.Identity, scale=w2f[:, d, 0:1], bias=c0[:, d, :])
+            if (s, d) in V_P0:
+                nc.vector.tensor_scalar(out=dst, in0=h[:, 0:n], scalar1=w2f[:, d, 0:1], scalar2=c0[:, d, :],
+                                        op0=ALU.mult, op1=ALU.add)
+            else:
+                nc.scalar.activation(out=dst, in_=h[:, 0:n], func=ACT.Identity, scale=w2f[:, d, 0:1], bias=c0[:, d, :])
             if t0 == 0:
                 seg = ys[b][:, d, 0:n - 1]
                 src = h[:, 1:n]
@@ -256,28 +261,36 @@ def tile_cvim_pa_kernel(tc, x, w1, b1, w2, b2, out_0, out_1):
 
         NS = len(SUBS)
         steps = [(s, d) for s in range(NS) for d in range(NDT)]
+        NST = len(steps)
         prep(1)
         hq = [mm(0, 0), mm(0, 1)]
-        for i in range(len(steps) + LAG):
-            if i + 2 < len(steps):
+        ready = [(4 * s + 3 + LAG, k) for s in range(NS - 1) for k in SUBS[s][3]]
+        group = []
+        nx = 0
+        for i in range(NST + LAG):
+            if i + 2 < NST:
                 hq.append(mm(steps[i + 2][0], steps[i + 2][1]))
-            if i < len(steps):
+            if i < NST:
                 s, d = steps[i]
                 conv(s, d, hq[i])
                 if s == 0 and d == 1:
                     prep(2)
                 if s == 0 and d == 3:
                     prep(3)
-            if i >= LAG:
-                s, d = steps[i - LAG]
-                tiles = SUBS[s][3]
-                for k in tiles:
-                    blocks(k, d)
-                if s > 0 and d == 1:
-                    finish(SUBS[s - 1][3])
-                if d == NDT - 1 and s < NS - 1:
-                    for k in tiles:
-                        leave(k)
+            for n in range(2):
+                if nx < len(ready) and ready[nx][0] <= i:
+                    k = ready[nx][1]
+                    nx += 1
+                    for d in range(NDT):
+                        blocks(k, d)
+                    leave(k)
+                    group.append(k)
+            if len(group) >= 3 or (group and nx == len(ready)):
+                finish(tuple(group))
+                group = []
+            if i - LAG >= NST - NDT:
+                for k in SUBS[NS - 1][3]:
+                    blocks(k, steps[i - LAG][1])
         for k in (11, 12, 13):
             leave(k)
         finish((11, 12, 13))

@@ -23,12 +23,12 @@ OFF0 = 8
 FLOPS = 2 * B * T * C * C + 2 * KW * B * T * C
 
 WARM = 6
-LAG = 2
+LAG = 1
 STREAM = True
 HB = 3
 TPB = 5
 S_CAST = (12, 14)
-V_P0 = ((1, 1),)
+V_P0 = ((0, 1), (1, 1), (2, 1))
 PREP_ENG = ("", "vs", "ss", "ss")
 G_SLOT = {0: 0, 2: 1}
 SUBS = (
@@ -198,10 +198,10 @@ def tile_cvim_pa_kernel(tc, x, w1, b1, w2, b2, out_0, out_1):
                 nc.scalar.activation(out=hs[:, 0:n], in_=h[:, 0:n], func=ACT.Identity, scale=1.0, bias=b1f[:, d, :])
                 nc.vector.tensor_scalar(out=ys[b][:, d, t0:t0 + n], in0=h[:, 0:n], scalar1=w2f[:, d, 1:2],
                                         scalar2=c1p[:, d, :], op0=ALU.mult, op1=ALU.add)
-                nc.gpsimd.tensor_scalar(out=dst, in0=hs[:, 0:n], scalar1=w2f[:, d, 0:1], scalar2=zt[:, 0:1],
+                nc.gpsimd.tensor_scalar(out=dst, in0=hs[:, 0:n], scalar1=w2f[:, d, 0:1], scalar2=0.0,
                                         op0=ALU.mult, op1=ALU.add)
                 nc.gpsimd.tensor_scalar(out=p2s[b][:, G_SLOT[d], t0:t0 + n], in0=hs[:, 0:n], scalar1=w2f[:, d, 2:3],
-                                        scalar2=zt[:, 0:1], op0=ALU.mult, op1=ALU.add)
+                                        scalar2=0.0, op0=ALU.mult, op1=ALU.add)
                 return
             nc.scalar.activation(out=ys[b][:, d, t0:t0 + n], in_=h[:, 0:n], func=ACT.Identity,
                                  scale=w2f[:, d, 1:2], bias=c1[:, d, :])

@@ -25,9 +25,9 @@ FLOPS = 2 * B * T * C * C + 2 * KW * B * T * C
 WARM = 6
 LAG = 1
 STREAM = True
-HB = 3
-TPB = 5
-S_CAST = (12, 14)
+HB = 4
+TPB = 4
+S_CAST = (12, 15)
 V_P0 = ((0, 1), (1, 1), (2, 1))
 PREP_ENG = ("", "vs", "ss", "ss")
 G_SLOT = {0: 0, 2: 1}
@@ -224,7 +224,10 @@ def tile_cvim_pa_kernel(tc, x, w1, b1, w2, b2, out_0, out_1):
         def blocks(k, d):
             b, t0 = divmod(k * P, T)
             if d == 0:
-                yos[k] = psum.tile([P, C], F32, tag="tp", bufs=TPB, name="yo")
+                if k == 15:
+                    yos[k] = psum.tile([P, C], F32, tag="h", bufs=HB, name="yo")
+                else:
+                    yos[k] = psum.tile([P, C], F32, tag="tp", bufs=TPB, name="yo")
             dst = yos[k][:, d * P:(d + 1) * P]
             st = OFF0 + t0 - 1
             nc.tensor.matmul(dst, lhsT=p0s[b][:, d, st:st + P], rhs=ident[:], is_transpose=True, start=True, stop=False)
@@ -263,13 +266,13 @@ def tile_cvim_pa_kernel(tc, x, w1, b1, w2, b2, out_0, out_1):
         steps = [(s, d) for s in range(NS) for d in range(NDT)]
         NST = len(steps)
         prep(1)
-        hq = [mm(0, 0), mm(0, 1)]
+        hq = [mm(0, 0), mm(0, 1), mm(0, 2)]
         ready = [(4 * s + 3 + LAG, k) for s in range(NS - 1) for k in SUBS[s][3]]
         group = []
         nx = 0
         for i in range(NST + LAG):
-            if i + 2 < NST:
-                hq.append(mm(steps[i + 2][0], steps[i + 2][1]))
+            if i + 3 < NST:
+                hq.append(mm(steps[i + 3][0], steps[i + 3][1]))
             if i < NST:
                 s, d = steps[i]
                 conv(s, d, hq[i])

@@ -271,15 +271,6 @@ def tile_cvim_pa_kernel(tc, x, w1, b1, w2, b2, out_0, out_1):
         group = []
         nx = 0
         for i in range(NST + LAG):
-            if i + 3 < NST:
-                hq.append(mm(steps[i + 3][0], steps[i + 3][1]))
-            if i < NST:
-                s, d = steps[i]
-                conv(s, d, hq[i])
-                if s == 0 and d == 1:
-                    prep(2)
-                if s == 0 and d == 3:
-                    prep(3)
             for n in range(2):
                 if nx < len(ready) and ready[nx][0] <= i:
                     k = ready[nx][1]
@@ -288,6 +279,16 @@ def tile_cvim_pa_kernel(tc, x, w1, b1, w2, b2, out_0, out_1):
                         blocks(k, d)
                     leave(k)
                     group.append(k)
+                if n == 0:
+                    if i + 3 < NST:
+                        hq.append(mm(steps[i + 3][0], steps[i + 3][1]))
+                    if i < NST:
+                        s, d = steps[i]
+                        conv(s, d, hq[i])
+                        if s == 0 and d == 1:
+                            prep(2)
+                        if s == 0 and d == 3:
+                            prep(3)
             if len(group) >= 3 or (group and nx == len(ready)):
                 finish(tuple(group))
                 group = []

@@ -22,7 +22,7 @@ PITCH = 1040
 OFF0 = 8
 FLOPS = 2 * B * T * C * C + 2 * KW * B * T * C
 
-WARM = 6
+WARM = 3
 LAG = 1
 STREAM = True
 HB = 4
@@ -31,6 +31,7 @@ S_CAST = (12, 15)
 V_P0 = ((0, 1), (1, 1), (2, 1))
 PREP_ENG = ("", "vs", "ss", "ss")
 G_SLOT = {0: 0, 2: 1}
+G_CENTRE = ((2, 2), (3, 0))
 SUBS = (
     (0, 0, 512, (0, 1, 2)),
     (0, 512, 512, (3, 4, 5, 6, 7)),
@@ -196,8 +197,12 @@ def tile_cvim_pa_kernel(tc, x, w1, b1, w2, b2, out_0, out_1):
             if d in G_SLOT:
                 hs = work.tile([P, CH], F32, tag="hs", bufs=4, name="hs")
                 nc.scalar.activation(out=hs[:, 0:n], in_=h[:, 0:n], func=ACT.Identity, scale=1.0, bias=b1f[:, d, :])
-                nc.vector.tensor_scalar(out=ys[b][:, d, t0:t0 + n], in0=h[:, 0:n], scalar1=w2f[:, d, 1:2],
-                                        scalar2=c1p[:, d, :], op0=ALU.mult, op1=ALU.add)
+                if (s, d) in G_CENTRE:
+                    nc.gpsimd.tensor_scalar(out=ys[b][:, d, t0:t0 + n], in0=hs[:, 0:n], scalar1=w2f[:, d, 1:2],
+                                            scalar2=b2f[:, d, :], op0=ALU.mult, op1=ALU.add)
+                else:
+                    nc.vector.tensor_scalar(out=ys[b][:, d, t0:t0 + n], in0=h[:, 0:n], scalar1=w2f[:, d, 1:2],
+                                            scalar2=c1p[:, d, :], op0=ALU.mult, op1=ALU.add)
                 nc.gpsimd.tensor_scalar(out=dst, in0=hs[:, 0:n], scalar1=w2f[:, d, 0:1], scalar2=0.0,
                                         op0=ALU.mult, op1=ALU.add)
                 nc.gpsimd.tensor_scalar(out=p2s[b][:, G_SLOT[d], t0:t0 + n], in0=hs[:, 0:n], scalar1=w2f[:, d, 2:3],

@@ -28,10 +28,10 @@ STREAM = True
 HB = 4
 TPB = 4
 S_CAST = (12, 15)
-V_P0 = ((0, 1), (1, 1), (2, 1))
+V_P0 = ((0, 1), (0, 3), (1, 1), (1, 3), (2, 1))
 PREP_ENG = ("", "vs", "ss", "ss")
 G_SLOT = {0: 0, 2: 1}
-G_CENTRE = ((2, 2), (3, 0))
+G_CENTRE = ((0, 0), (1, 0), (2, 2), (3, 0))
 SUBS = (
     (0, 0, 512, (0, 1, 2)),
     (0, 512, 512, (3, 4, 5, 6, 7)),

from contextlib import ExitStack

import concourse.mybir as mybir
from concourse.masks import make_identity

F32 = mybir.dt.float32
BF16 = mybir.dt.bfloat16
U32 = mybir.dt.uint32
U8 = mybir.dt.uint8
FP8X4 = mybir.dt.float8_e4m3fn_x4
FP8 = mybir.dt.float8_e4m3fn
ALU = mybir.AluOpType
ACT = mybir.ActivationFunctionType
AX = mybir.AxisListType

B, T, C, KW = 2, 1024, 512, 3
P = 128
NDT = C // P
CH = 512
NCH = B * T // CH
PITCH = 1040
OFF0 = 8
FLOPS = 2 * B * T * C * C + 2 * KW * B * T * C

WARM = 3
LAG = 1
STREAM = True
HB = 4
TPB = 4
S_CAST = (12, 15)
V_P0 = ((0, 1), (0, 3), (1, 1), (1, 3), (2, 1))
PREP_ENG = ("", "vs", "ss", "ss")
G_SLOT = {0: 0, 2: 1}
G_CENTRE = ((0, 0), (1, 0), (2, 2), (3, 0))
SUBS = (
    (0, 0, 512, (0, 1, 2)),
    (0, 512, 512, (3, 4, 5, 6, 7)),
    (1, 0, 512, (8, 9, 10)),
    (1, 512, 512, (11, 12, 13, 14, 15)),
)


def tile_cvim_pa_kernel(tc, x, w1, b1, w2, b2, out_0, out_1):
    nc = tc.nc
    xf = x.flatten_outer_dims()
    o0f = out_0.flatten_outer_dims()
    o1f = out_1.flatten_outer_dims()

    with ExitStack() as ctx:
        keep = ctx.enter_context(tc.tile_pool(name="keep", bufs=1))
        work = ctx.enter_context(tc.tile_pool(name="work", bufs=4))
        psum = ctx.enter_context(tc.psum_pool(name="psum", bufs=2))

        def load_w(h):
            raw = keep.tile([P, 2, C], BF16, name="wraw%d" % h)
            nc.sync.dma_start(out=raw[:], in_=w1.rearrange("(p c) k -> p c k", c=NDT)[:, 2 * h:2 * h + 2, :])
            return raw

        def load_x(i):
            raw = keep.tile([P, 2, C], BF16, name="xraw%d" % i)
            nc.sync.dma_start(out=raw[:], in_=xf[256 * i:256 * (i + 1), :].rearrange("(p a) k -> p a k", a=2))
            return raw

        w_raw = [None, None]
        x_raw = [None] * 8
        x_raw[0] = load_x(0)
        w_raw[0] = load_w(0)
        x_raw[1] = load_x(1)
        w_raw[1] = load_w(1)

        b1c = keep.tile([P, NDT, 1], BF16, name="b1c")
        b2c = keep.tile([P, NDT, 1], BF16, name="b2c")
        w2c = keep.tile([P, NDT, KW], BF16, name="w2c")
        nc.scalar.dma_start(out=b1c[:], in_=b1.rearrange("(p c o) -> p c o", c=NDT, o=1))
        nc.scalar.dma_start(out=w2c[:], in_=w2.rearrange("(p c) j -> p c j", c=NDT))
        nc.scalar.dma_start(out=b2c[:], in_=b2.rearrange("(p c o) -> p c o", c=NDT, o=1))
        for i in range(2, 8):
            x_raw[i] = load_x(i)

        if WARM:
            wz = keep.tile([P, CH], BF16, name="wz")
            nc.vector.memset(wz[:], 0.0)
            dm = psum.tile([P, CH], F32, tag="tp", bufs=TPB, name="dm")
            for i in range(WARM):
                nc.tensor.matmul(dm[:], lhsT=wz[:, 0:P], rhs=wz[:], start=True, stop=True)

        ident = keep.tile([P, P], F32, name="ident")
        make_identity(nc, ident[:])
        zt = keep.tile([P, 1], F32, name="zt")
        nc.vector.memset(zt[:], 0.0)
        junk = keep.tile([P, 1], F32, name="junk")
        nc.scalar.activation(out=junk[:], in_=zt[:], func=ACT.Identity, bias=zt[:, 0:1], scale=1.0)

        b1f = keep.tile([P, NDT, 1], F32, name="b1f")
        b2f = keep.tile([P, NDT, 1], F32, name="b2f")
        w2f = keep.tile([P, NDT, KW], F32, name="w2f")
        nc.vector.tensor_copy(out=b1f[:], in_=b1c[:])
        nc.vector.tensor_copy(out=w2f[:], in_=w2c[:])
        nc.vector.tensor_copy(out=b2f[:], in_=b2c[:])
        c0 = keep.tile([P, NDT, 1], F32, name="c0")
        w12 = keep.tile([P, NDT, 1], F32, name="w12")
        c1a = keep.tile([P, NDT, 1], F32, name="c1a")
        c1 = keep.tile([P, NDT, 1], F32, name="c1")
        f2 = keep.tile([P, NDT, 1], F32, name="f2")
        nc.vector.tensor_tensor(out=c0[:], in0=w2f[:, :, 0:1], in1=b1f[:], op=ALU.mult)
        nc.vector.tensor_tensor(out=w12[:], in0=w2f[:, :, 1:2], in1=w2f[:, :, 2:3], op=ALU.add)
        nc.vector.tensor_tensor(out=c1a[:], in0=w12[:], in1=b1f[:], op=ALU.mult)
        nc.vector.tensor_tensor(out=c1[:], in0=c1a[:], in1=b2f[:], op=ALU.add)
        nc.vector.scalar_tensor_tensor(out=f2[:], in0=w2f[:, :, 2:3], scalar=-1.0, in1=b1f[:], op0=ALU.mult, op1=ALU.mult)
        c1p = keep.tile([P, NDT, 1], F32, name="c1p")
        nc.vector.tensor_tensor(out=c1p[:], in0=c1[:], in1=f2[:], op=ALU.add)

        ys = [keep.tile([P, NDT, T], F32, name="y%d" % b) for b in range(B)]
        p0s = [keep.tile([P, NDT, PITCH], F32, name="p0_%d" % b) for b in range(B)]
        p2s = [keep.tile([P, max(1, len(G_SLOT)), T + 8], F32, name="p2_%d" % b) for b in range(B)]
        for b in range(B):
            nc.gpsimd.memset(p0s[b][:, :, OFF0 - 1:OFF0], 0.0)
            nc.gpsimd.memset(p2s[b][:, :, T:T + 1], 0.0)

        fixt = keep.tile([P, NDT, P], F32, name="fixt")
        nc.gpsimd.memset(fixt[:], 0.0)
        nc.vector.tensor_copy(out=fixt[:, :, P - 1:P], in_=f2[:])

        am = keep.tile([P, 16], F32, name="am")
        rc = keep.tile([P, 16], F32, name="rc")
        rs = keep.tile([P, 16], F32, name="rs")

        wq = keep.tile([P, CH], U32, name="wq", align_bytes=64)
        ws = keep.tile([P, CH], U8, name="ws", align_bytes=64)
        xq = [keep.tile([P, CH], U32, name="xq%d" % c, align_bytes=64) for c in range(NCH)]
        xs = [keep.tile([P, CH], U8, name="xs%d" % c, align_bytes=64) for c in range(NCH)]

        def turn(raw):
            words = raw[:].bitcast(F32)
            tin = psum.tile([P, 2, 2, P], F32, tag="tp", bufs=TPB, name="tin")
            for a in range(2):
                for u in range(2):
                    nc.tensor.transpose(tin[:, a, u, :], words[:, a, u:C // 2:2], ident[:])
            return tin

        def gather(tin, dst, eng, order):
            if order == "w":
                o = dst.rearrange("p (a r u) -> p a r u", a=2, u=2)
                i = tin[:].rearrange("p a u r -> p a r u")
            else:
                o = dst.rearrange("p (r a u) -> p r a u", a=2, u=2)
                i = tin[:].rearrange("p a u r -> p r a u")
            if eng == "s":
                nc.scalar.copy(out=o, in_=i)
            else:
                nc.vector.tensor_copy(out=o, in_=i)

        def quant(g, codes, scales):
            nc.vector.quantize_mx(out=codes.bitcast(FP8X4), scales=scales, in_=g.bitcast(BF16))

        gw = work.tile([P, 2, CH], F32, tag="g", bufs=3, name="gw", align_bytes=64)
        g0 = work.tile([P, 2, CH], F32, tag="g", bufs=3, name="g0", align_bytes=64)
        ctx.enter_context(tc.manual_schedule(engines={mybir.EngineType.PE}))
        tx0 = turn(x_raw[0])
        tw0 = turn(w_raw[0])
        gather(tx0, g0[:, 0, :], "v", "x")
        gather(tw0, gw[:, 0, :], "s", "w")
        tx1 = turn(x_raw[1])
        tw1 = turn(w_raw[1])
        quant(g0[:, 0, :], xq[0][:, 0:256], xs[0][:, 0:256])
        quant(gw[:, 0, :], wq[:, 0:256], ws[:, 0:256])
        gather(tx1, g0[:, 1, :], "s", "x")
        gather(tw1, gw[:, 1, :], "s", "w")
        quant(g0[:, 1, :], xq[0][:, 256:512], xs[0][:, 256:512])
        quant(gw[:, 1, :], wq[:, 256:512], ws[:, 256:512])

        def prep(c):
            g = work.tile([P, 2, CH], F32, tag="g", bufs=3, name="g", align_bytes=64)
            tins = [turn(x_raw[2 * c]), turn(x_raw[2 * c + 1])]
            for h in range(2):
                gather(tins[h], g[:, h, :], PREP_ENG[c][h], "x")
            quant(g[:].rearrange("p h w -> p (h w)"), xq[c][:], xs[c][:])

        def mm(s, d):
            b, t0, n, tiles = SUBS[s]
            c, col = divmod(b * T + t0, CH)
            h = psum.tile([P, CH], F32, tag="h", bufs=HB, name="h")
            nc.tensor.matmul_mx(
                out=h[:, 0:n],
                lhsT=wq[:, d * P:(d + 1) * P].bitcast(FP8X4),
                lhsT_scale=ws[:, d * P:(d + 1) * P],
                rhs=xq[c][:, col:col + n].bitcast(FP8X4),
                rhs_scale=xs[c][:, col:col + n],
                start=True,
                stop=True,
            )
            return h

        def conv(s, d, h):
            b, t0, n, tiles = SUBS[s]
            dst = p0s[b][:, d, OFF0 + t0:OFF0 + t0 + n]
            if d in G_SLOT:
                hs = work.tile([P, CH], F32, tag="hs", bufs=4, name="hs")
                nc.scalar.activation(out=hs[:, 0:n], in_=h[:, 0:n], func=ACT.Identity, scale=1.0, bias=b1f[:, d, :])
                if (s, d) in G_CENTRE:
                    nc.gpsimd.tensor_scalar(out=ys[b][:, d, t0:t0 + n], in0=hs[:, 0:n], scalar1=w2f[:, d, 1:2],
                                            scalar2=b2f[:, d, :], op0=ALU.mult, op1=ALU.add)
                else:
                    nc.vector.tensor_scalar(out=ys[b][:, d, t0:t0 + n], in0=h[:, 0:n], scalar1=w2f[:, d, 1:2],
                                            scalar2=c1p[:, d, :], op0=ALU.mult, op1=ALU.add)
                nc.gpsimd.tensor_scalar(out=dst, in0=hs[:, 0:n], scalar1=w2f[:, d, 0:1], scalar2=0.0,
                                        op0=ALU.mult, op1=ALU.add)
                nc.gpsimd.tensor_scalar(out=p2s[b][:, G_SLOT[d], t0:t0 + n], in0=hs[:, 0:n], scalar1=w2f[:, d, 2:3],
                                        scalar2=0.0, op0=ALU.mult, op1=ALU.add)
                return
            nc.scalar.activation(out=ys[b][:, d, t0:t0 + n], in_=h[:, 0:n], func=ACT.Identity,
                                 scale=w2f[:, d, 1:2], bias=c1[:, d, :])
            if (s, d) in V_P0:
                nc.vector.tensor_scalar(out=dst, in0=h[:, 0:n], scalar1=w2f[:, d, 0:1], scalar2=c0[:, d, :],
                                        op0=ALU.mult, op1=ALU.add)
            else:
                nc.scalar.activation(out=dst, in_=h[:, 0:n], func=ACT.Identity, scale=w2f[:, d, 0:1], bias=c0[:, d, :])
            if t0 == 0:
                seg = ys[b][:, d, 0:n - 1]
                src = h[:, 1:n]
            else:
                seg = ys[b][:, d, t0 - 1:t0 + n - 1]
                src = h[:, 0:n]
            nc.vector.scalar_tensor_tensor(out=seg, in0=src, scalar=w2f[:, d, 2:3], in1=seg, op0=ALU.mult, op1=ALU.add)

        yos = [None] * 16
        o0s = [None] * 16

        def blocks(k, d):
            b, t0 = divmod(k * P, T)
            if d == 0:
                if k == 15:
                    yos[k] = psum.tile([P, C], F32, tag="h", bufs=HB, name="yo")
                else:
                    yos[k] = psum.tile([P, C], F32, tag="tp", bufs=TPB, name="yo")
            dst = yos[k][:, d * P:(d + 1) * P]
            st = OFF0 + t0 - 1
            nc.tensor.matmul(dst, lhsT=p0s[b][:, d, st:st + P], rhs=ident[:], is_transpose=True, start=True, stop=False)
            if d in G_SLOT:
                nc.tensor.matmul(dst, lhsT=ys[b][:, d, t0:t0 + P], rhs=ident[:], is_transpose=True, start=False, stop=False)
                nc.tensor.matmul(dst, lhsT=p2s[b][:, G_SLOT[d], t0 + 1:t0 + 1 + P], rhs=ident[:], is_transpose=True,
                                 start=False, stop=True)
                return
            last = t0 + P == T
            nc.tensor.matmul(dst, lhsT=ys[b][:, d, t0:t0 + P], rhs=ident[:], is_transpose=True, start=False, stop=not last)
            if last:
                nc.tensor.matmul(dst, lhsT=fixt[:, d, :], rhs=ident[:], is_transpose=True, start=False, stop=True)

        def leave(k):
            o0 = work.tile([P, C], F32, tag="o0", bufs=10, name="o0")
            nc.scalar.copy(out=o0[:].rearrange("p (m c) -> p m c", c=NDT), in_=yos[k][:].rearrange("p (c m) -> p m c", c=NDT))
            nc.sync.dma_start(out=o0f[k * P:(k + 1) * P, :], in_=o0[:])
            nc.vector.tensor_reduce(out=am[:, k:k + 1], in_=o0[:], axis=AX.X, op=ALU.max, apply_absolute_value=True)
            o0s[k] = o0

        def finish(tiles):
            k0, k1 = tiles[0], tiles[-1] + 1
            nc.vector.reciprocal(out=rc[:, k0:k1], in_=am[:, k0:k1])
            nc.vector.tensor_scalar(out=rs[:, k0:k1], in0=rc[:, k0:k1], scalar1=448.0, scalar2=None, op0=ALU.mult)
            for k in tiles:
                o8 = work.tile([P, C], FP8, tag="o8", bufs=6, name="o8")
                if k in S_CAST:
                    nc.scalar.activation(out=o8[:], in_=o0s[k][:], func=ACT.Identity, scale=rs[:, k:k + 1],
                                         bias=zt[:, 0:1], saturate=False)
                else:
                    nc.vector.tensor_scalar(out=o8[:], in0=o0s[k][:], scalar1=rs[:, k:k + 1], scalar2=None,
                                            op0=ALU.mult, saturate=False)
                nc.sync.dma_start(out=o1f[k * P:(k + 1) * P, :], in_=o8[:].bitcast(U8))

        NS = len(SUBS)
        steps = [(s, d) for s in range(NS) for d in range(NDT)]
        NST = len(steps)
        prep(1)
        hq = [mm(0, 0), mm(0, 1), mm(0, 2)]
        ready = [(4 * s + 3 + LAG, k) for s in range(NS - 1) for k in SUBS[s][3]]
        group = []
        nx = 0
        for i in range(NST + LAG):
            for n in range(2):
                if nx < len(ready) and ready[nx][0] <= i:
                    k = ready[nx][1]
                    nx += 1
                    for d in range(NDT):
                        blocks(k, d)
                    leave(k)
                    group.append(k)
                if n == 0:
                    if i + 3 < NST:
                        hq.append(mm(steps[i + 3][0], steps[i + 3][1]))
                    if i < NST:
                        s, d = steps[i]
                        conv(s, d, hq[i])
                        if s == 0 and d == 1:
                            prep(2)
                        if s == 0 and d == 3:
                            prep(3)
            if len(group) >= 3 or (group and nx == len(ready)):
                finish(tuple(group))
                group = []
            if i - LAG >= NST - NDT:
                for k in SUBS[NS - 1][3]:
                    blocks(k, steps[i - LAG][1])
        for k in (11, 12, 13):
            leave(k)
        finish((11, 12, 13))
        for k in (14, 15):
            leave(k)
        finish((14, 15))
